import numpy as np
import ml_dtypes


def mxq(x, axis, fmt="e4m3"):
    dtype, down = {"e4m3": (ml_dtypes.float8_e4m3fn, 7), "e5m2": (ml_dtypes.float8_e5m2, 14)}[fmt]
    v = np.moveaxis(np.asarray(x, np.float32).astype(ml_dtypes.bfloat16).astype(np.float64), axis, -1)
    blocks = v.reshape(v.shape[:-1] + (-1, 32))
    amax = np.abs(blocks).max(-1, keepdims=True)
    byte = np.maximum(np.where(amax > 0, np.frexp(amax)[1] - 1 + 127, 0) - down, 1)
    scale = np.exp2(byte - 127.0)
    codes = (blocks / scale).astype(np.float32).astype(dtype).astype(np.float64)
    return np.moveaxis((codes * scale).reshape(v.shape), -1, axis)


WIDE = False


def mx_kscale(k):
    if not WIDE:
        return np.ones(k)
    levels = np.array([10, -10, 5, -5, 0])
    if k % 512:
        return np.exp2(np.random.permutation(np.resize(levels, k // 32))).repeat(32)
    a = np.empty((k // 512, 16))
    for p in range(k // 512):
        a[p, :8] = np.random.permutation(np.resize(levels, 8))
        for g in range(8):
            far = levels[np.abs(levels - a[p, g]) >= 10]
            a[p, g + 8] = far[np.random.randint(len(far))]
    return np.exp2(a.ravel()).repeat(32)


BF16 = ml_dtypes.bfloat16


def bf(x):
    return np.asarray(x, np.float32).astype(BF16)


def f64(x):
    return np.asarray(x).astype(np.float64)


B, IN, M, OUT = 1024, 1024, 512, 512
F = 2 * M
EPS = 1e-12


def draw0():
    s, t = mx_kscale(IN), mx_kscale(F)
    return {"x": bf(np.random.standard_normal((B, IN)) * s),
            "W1": bf(np.random.standard_normal((IN, F)) / np.sqrt(IN) / s[:, None] * t),
            "b1": bf(np.random.standard_normal(F) * 0.1 * t),
            "W2": bf(np.random.standard_normal((F, M)) / np.sqrt(F) / t[:, None]),
            "b2": bf(np.random.standard_normal(M) * 0.3)}


def core(x, W1, b1, W2, b2):
    h = np.maximum((mxq(f64(x), 1, "e4m3") @ mxq(f64(W1), 0, "e4m3")) + f64(b1), 0.0)
    v = (mxq(h, 1, "e4m3") @ mxq(f64(W2), 0, "e4m3")) + f64(b2)
    norm = np.sqrt(np.sum(v * v, axis=-1, keepdims=True))
    return v / np.maximum(norm, EPS)


def e4m3fn_bytes(y):
    return np.clip(np.asarray(y, np.float64), -448.0, 448.0).astype(np.float32).astype(ml_dtypes.float8_e4m3fn).view(np.uint8)


def e4m3fn_values(b):
    return np.asarray(b, np.uint8).view(ml_dtypes.float8_e4m3fn).astype(np.float64)


def setup_inputs():
    d = draw0()
    x0 = np.asarray(d['x']).astype(np.float64)
    s = (np.max(np.abs(x0), axis=(0,), keepdims=True) / 448.0).astype(np.float32)
    out = {}
    for k, v in d.items():
        if k == 'x':
            out['x_bytes'] = e4m3fn_bytes(x0 / s.astype(np.float64))
            out['x_scale'] = s
        else:
            out[k] = v
    return out


def reference(x_bytes, x_scale, W1, b1, W2, b2):
    return core(e4m3fn_values(x_bytes) * x_scale.astype(np.float64), W1, b1, W2, b2)

@@ -1,0 +1,454 @@
+from contextlib import ExitStack
+
+import concourse.mybir as mybir
+from concourse.masks import make_identity
+
+B, IN, F, OUT = 1024, 1024, 1024, 512
+FLOPS = 2 * B * IN * F + 2 * B * F * OUT
+EPS = 1e-12
+
+F32 = mybir.dt.float32
+BF16 = mybir.dt.bfloat16
+U32 = mybir.dt.uint32
+U8 = mybir.dt.uint8
+FP8 = mybir.dt.float8_e4m3fn
+FP8X4 = mybir.dt.float8_e4m3fn_x4
+ACT = mybir.ActivationFunctionType
+ALU = mybir.AluOpType
+
+P = 128
+NT = 8
+CHUNKS = [(0, 2), (2, 4), (4, 6), (6, 8)]
+
+
+def tile_geometricmanifoldnetwork_pa_kernel(tc, x_bytes, x_scale, W1, b1, W2, b2, out):
+    nc = tc.nc
+    with ExitStack() as ctx:
+        keep = ctx.enter_context(tc.tile_pool(name="keep", bufs=1))
+        work = ctx.enter_context(tc.tile_pool(name="work", bufs=4))
+        ps_x = ctx.enter_context(tc.psum_pool(name="ps_x", bufs=2))
+        ps_h = ctx.enter_context(tc.psum_pool(name="ps_h", bufs=4))
+        ps_o = ctx.enter_context(tc.psum_pool(name="ps_o", bufs=2))
+
+        x_view = x_bytes.rearrange("(p n) k -> p n k", n=NT)
+        out_view = out.rearrange("(p n) m -> p n m", n=NT)
+
+
+        ident = keep.tile([P, P], F32, name="ident")
+        make_identity(nc, ident[:])
+        ident_b = keep.tile([P, P], BF16, name="ident_b")
+        make_identity(nc, ident_b[:])
+        one = keep.tile([P, 1], F32, name="one")
+        nc.vector.memset(one[:], 1.0)
+        eps = keep.tile([P, 1], F32, name="eps")
+        nc.scalar.activation(out=eps[:], in_=one[:], func=ACT.Sqrt, scale=EPS * EPS)
+        nchunk = [(b - a) * P for a, b in CHUNKS]
+
+        s_col = keep.tile([P, 8], F32, name="s_col")
+        b1_col = keep.tile([P, 2, 4], BF16, name="b1_col")
+        b2_col = keep.tile([P, 4], BF16, name="b2_col")
+        s_all = keep.tile([P, 128, 8], F32, name="s_all")
+        s_flat = s_all[:].rearrange("q p c -> q (p c)")
+        b2_all = keep.tile([P, OUT], F32, name="b2_all")
+        T = {}
+
+        def load_s():
+            nc.sync.dma_start(out=s_col[:], in_=x_scale.rearrange("o (p c) -> p (o c)", c=8))
+
+        def load_b():
+            nc.sync.dma_start(out=b1_col[:], in_=b1.rearrange("(g p t) -> p g t", p=P, t=4))
+            nc.sync.dma_start(out=b2_col[:], in_=b2.rearrange("(p c) -> p c", c=4))
+
+        def load_w1(g, G):
+            t = keep.tile([P, 4, 512], BF16, name=f"w1_raw_{g}_{G}")
+            nc.sync.dma_start(
+                out=t[:],
+                in_=W1[512 * g : 512 * g + 512, 512 * G : 512 * G + 512].rearrange("(p j) c -> p j c", j=4),
+            )
+            T["w1_raw", g, G] = t
+
+        def load_x(c):
+            n0, n1 = CHUNKS[c]
+            t = keep.tile([P, n1 - n0, IN], U8, name=f"x_raw_{c}")
+            nc.sync.dma_start(out=t[:], in_=x_view[:, n0:n1, :])
+            T["x_raw", c] = t
+
+        def load_w2(G):
+            t = keep.tile([P, 4, 512], BF16, name=f"w2_raw_{G}")
+            nc.sync.dma_start(out=t[:], in_=W2[512 * G : 512 * G + 512, :].rearrange("(p j) c -> p j c", j=4))
+            T["w2_raw", G] = t
+
+        def copy(eng, dst, src):
+            if eng == "V":
+                nc.vector.tensor_copy(out=dst, in_=src)
+            elif eng == "S":
+                nc.scalar.copy(out=dst, in_=src)
+            else:
+                nc.gpsimd.tensor_scalar(out=dst, in0=src, scalar1=1.0, scalar2=0.0, op0=ALU.mult, op1=ALU.add)
+
+        def s_turn():
+            for h in range(2):
+                bank = ps_x.tile([P, 4, P], F32, name="bank_x")
+                for c in range(4):
+                    nc.tensor.transpose(
+                        bank[:, c, :], s_col[:, 4 * h + c : 4 * h + c + 1].to_broadcast([P, P]), ident[:]
+                    )
+                T["s_bank", h] = bank
+
+        def s_out(h, eng):
+            copy(eng, s_all[:, :, 4 * h : 4 * h + 4], T["s_bank", h][:].rearrange("q c p -> q p c"))
+
+        def w1_inter(g, G, h, eng):
+            if ("w1_grp", g, G) not in T:
+                T["w1_grp", g, G] = keep.tile([P, 2048], BF16, name=f"w1_grp_{g}_{G}", align_bytes=64)
+            m = slice(64 * h, 64 * h + 64)
+            dst = T["w1_grp", g, G][:].rearrange("p (t m j) -> p m j t", t=4, j=4)[:, m]
+            src = T["w1_raw", g, G][:].rearrange("p j (m t) -> p m j t", t=4)[:, m]
+            copy(eng, dst, src)
+
+        def quantize(key, words, src):
+            code = keep.tile([P, words], U32, name="code_" + key, align_bytes=64)
+            scl = keep.tile([P, words], U8, name="scl_" + key, align_bytes=64)
+            nc.vector.quantize_mx(out=code[:].bitcast(FP8X4), scales=scl[:], in_=src)
+            return code, scl
+
+        def w1_quant(g, G):
+            T["w1", g, G] = quantize(f"w1_{g}_{G}", 512, T["w1_grp", g, G][:])
+
+        def w2_inter(G, h, eng):
+            if ("w2_grp", G) not in T:
+                T["w2_grp", G] = keep.tile([P, 512, 4], BF16, name=f"w2_grp_{G}", align_bytes=64)
+            c = slice(256 * h, 256 * h + 256)
+            dst = T["w2_grp", G][:, c, :].rearrange("p (c i) t -> p c t i", i=4)
+            src = T["w2_raw", G][:, :, c].rearrange("p t (c i) -> p c t i", i=4)
+            copy(eng, dst, src)
+
+        def w2_quant(G):
+            T["w2", G] = quantize(f"w2_{G}", 512, T["w2_grp", G][:].rearrange("p c t -> p (c t)"))
+
+        def prod(c, i):
+            t = work.tile([P, IN], BF16, name="x_prod")
+            nc.vector.tensor_tensor(out=t[:], in0=T["x_raw", c][:, i, :].bitcast(FP8), in1=s_flat, op=ALU.mult)
+            T["x_prod", c, i] = t
+
+        def turn(c, i):
+            words = T["x_prod", c, i][:].bitcast(F32)
+            bank = ps_x.tile([P, 2, 2, P], F32, name="bank_x")
+            for g in range(2):
+                for u in range(2):
+                    nc.tensor.transpose(bank[:, g, u, :], words[:, 256 * g + u : 256 * g + 256 : 2], ident[:])
+            T["x_bank", c, i] = bank
+
+        def x_out(c, i, eng):
+            if ("x_grp", c) not in T:
+                T["x_grp", c] = keep.tile([P, 2, nchunk[c], 4], BF16, name=f"x_grp_{c}", align_bytes=64)
+            dst = T["x_grp", c][:, :, P * i : P * i + P, :].bitcast(F32)
+            copy(eng, dst, T["x_bank", c, i][:].rearrange("p g u r -> p g r u"))
+
+        def x_quant(c):
+            T["x", c] = quantize(f"x_{c}", 2 * nchunk[c], T["x_grp", c][:].rearrange("p g n t -> p (g n t)"))
+
+        def stage1(c, G, t):
+            n = nchunk[c]
+            bank = ps_h.tile([P, 512], F32, name="bank_h")
+            for g in range(2):
+                w_code, w_scl = T["w1", g, G]
+                x_code, x_scl = T["x", c]
+                nc.tensor.matmul_mx(
+                    out=bank[:, :n],
+                    lhsT=w_code[:, P * t : P * t + P].bitcast(FP8X4),
+                    lhsT_scale=w_scl[:, P * t : P * t + P],
+                    rhs=x_code[:, g * n : g * n + n].bitcast(FP8X4),
+                    rhs_scale=x_scl[:, g * n : g * n + n],
+                    start=(g == 0),
+                    stop=(g == 1),
+                )
+            T["h_bank", c, G, t] = bank
+
+        def h_out(c, G, t, eng):
+            n = nchunk[c]
+            if ("h_plane", c, G) not in T:
+                T["h_plane", c, G] = work.tile([P, 4, n], BF16, name=f"h_plane_{n}")
+            dst = T["h_plane", c, G][:, t, :]
+            src = T["h_bank", c, G, t][:, :n]
+            bias = b1_col[:, G, t : t + 1]
+            if eng == "S":
+                nc.scalar.activation(out=dst, in_=src, func=ACT.Relu, bias=bias)
+            else:
+                nc.vector.tensor_scalar(out=dst, in0=src, scalar1=bias, scalar2=0.0, op0=ALU.add, op1=ALU.max)
+
+        def h_inter(c, G, eng):
+            t = work.tile([P, nchunk[c], 4], BF16, name=f"h_grp_{nchunk[c]}", align_bytes=64)
+            copy(
+                eng,
+                t[:].rearrange("p (c i) t -> p c t i", i=4),
+                T["h_plane", c, G][:].rearrange("p t (c i) -> p c t i", i=4),
+            )
+            T["h_grp", c, G] = t
+
+        def h_quant(c, G):
+            T["h", c, G] = quantize(f"h_{c}_{G}", nchunk[c], T["h_grp", c, G][:].rearrange("p n t -> p (n t)"))
+
+        def b2_spread():
+            bank = ps_o.tile([P, 4, P], F32, name="bank_o")
+            for c in range(4):
+                nc.tensor.matmul(
+                    bank[:, c, :], lhsT=b2_col[:, c : c + 1].to_broadcast([P, P]), rhs=ident_b[:], start=True, stop=True
+                )
+            T["b2_bank"] = bank
+
+        def b2_out(eng):
+            copy(eng, b2_all[:].rearrange("q (p c) -> q p c", c=4), T["b2_bank"][:].rearrange("q c p -> q p c"))
+
+        def stage2(c, i):
+            bank = ps_o.tile([P, OUT], F32, name="bank_o")
+            for G in range(2):
+                h_code, h_scl = T["h", c, G]
+                w_code, w_scl = T["w2", G]
+                nc.tensor.matmul_mx(
+                    out=bank[:],
+                    lhsT=h_code[:, P * i : P * i + P].bitcast(FP8X4),
+                    lhsT_scale=h_scl[:, P * i : P * i + P],
+                    rhs=w_code[:].bitcast(FP8X4),
+                    rhs_scale=w_scl[:],
+                    start=(G == 0),
+                    stop=(G == 1),
+                )
+            T["o_bank", c, i] = bank
+
+        def v_bias(c, i):
+            t = keep.tile([P, OUT], F32, name=f"v_{c}_{i}")
+            nc.vector.tensor_tensor(out=t[:], in0=T["o_bank", c, i][:], in1=b2_all[:], op=ALU.add)
+            T["v", c, i] = t
+
+        def v_square(c, i):
+            if ("ss", c) not in T:
+                T["ss", c] = keep.tile([P, nchunk[c] // P], F32, name=f"ss_{c}")
+            junk = work.tile([P, OUT], BF16, name="junk")
+            nc.scalar.activation(out=junk[:], in_=T["v", c, i][:], func=ACT.Square, accum_out=T["ss", c][:, i : i + 1])
+
+        def v_root(c):
+            T["nrm", c] = keep.tile([P, nchunk[c] // P], F32, name=f"nrm_{c}")
+            nc.scalar.activation(out=T["nrm", c][:], in_=T["ss", c][:], func=ACT.Sqrt)
+
+        def v_max(c):
+            T["mx", c] = keep.tile([P, nchunk[c] // P], F32, name=f"mx_{c}")
+            nc.vector.tensor_scalar(
+                out=T["mx", c][:], in0=T["nrm", c][:], scalar1=eps[:, 0:1], scalar2=None, op0=ALU.max
+            )
+
+        def v_recip(c):
+            T["rn", c] = keep.tile([P, nchunk[c] // P], F32, name=f"rn_{c}")
+            nc.vector.reciprocal(out=T["rn", c][:], in_=T["mx", c][:])
+
+        def v_mul(c, i, eng):
+            t = keep.tile([P, OUT], F32, name=f"res_{c}_{i}")
+            r = T["rn", c][:, i : i + 1]
+            v = T["v", c, i][:]
+            if eng == "V":
+                nc.vector.tensor_scalar(out=t[:], in0=v, scalar1=r, scalar2=None, op0=ALU.mult)
+            elif eng == "S":
+                nc.scalar.activation(out=t[:], in_=v, func=ACT.Copy, scale=r)
+            else:
+                nc.gpsimd.tensor_scalar(out=t[:], in0=v, scalar1=r, scalar2=1.0, op0=ALU.mult, op1=ALU.mult)
+            T["res", c, i] = t
+
+        def v_store(c, i):
+            nc.sync.dma_start(out=out_view[:, CHUNKS[c][0] + i, :], in_=T["res", c, i][:])
+
+        with tc.manual_schedule():
+            load_s()
+            load_x(0)
+            s_turn()
+            load_w1(0, 0)
+            s_out(0, "S")
+            load_w1(1, 1)
+            s_out(1, "V")
+            load_x(2)
+            prod(0, 1)
+            prod(0, 0)
+            load_x(1)
+            w1_inter(1, 1, 1, "V")
+            turn(0, 1)
+            w1_inter(0, 0, 0, "S")
+            w1_inter(0, 0, 1, "S")
+            load_w1(1, 0)
+            prod(1, 1)
+            w1_inter(1, 1, 0, "S")
+            load_w1(0, 1)
+            w1_inter(1, 0, 1, "S")
+            prod(2, 0)
+            turn(0, 0)
+            w1_quant(0, 0)
+            w1_inter(0, 1, 1, "S")
+            prod(1, 0)
+            x_out(0, 1, "S")
+            x_out(0, 0, "S")
+            w1_inter(1, 0, 0, "S")
+            turn(1, 0)
+            x_out(1, 0, "S")
+            w1_inter(0, 1, 0, "V")
+            load_w2(0)
+            turn(1, 1)
+            x_quant(0)
+            prod(2, 1)
+            x_out(1, 1, "S")
+            w1_quant(1, 0)
+            w2_inter(0, 0, "S")
+            w1_quant(0, 1)
+            turn(2, 0)
+            load_b()
+            stage1(0, 0, 3)
+            stage1(0, 0, 0)
+            x_quant(1)
+            stage1(0, 0, 1)
+            load_x(3)
+            h_out(0, 0, 3, "V")
+            h_out(0, 0, 0, "S")
+            w1_quant(1, 1)
+            stage1(0, 0, 2)
+            x_out(2, 0, "S")
+            stage1(1, 0, 2)
+            h_out(1, 0, 2, "V")
+            stage1(1, 0, 1)
+            h_out(0, 0, 2, "S")
+            load_w2(1)
+            turn(2, 1)
+            h_out(0, 0, 1, "S")
+            w2_inter(0, 1, "S")
+            stage1(1, 1, 1)
+            h_out(1, 0, 1, "S")
+            stage1(0, 1, 0)
+            h_out(1, 1, 1, "S")
+            stage1(0, 1, 1)
+            prod(3, 1)
+            w2_inter(1, 0, "V")
+            h_out(0, 1, 1, "V")
+            h_out(0, 1, 0, "S")
+            stage1(0, 1, 2)
+            h_inter(0, 0, "V")
+            stage1(1, 1, 0)
+            w2_quant(0)
+            prod(3, 0)
+            h_out(0, 1, 2, "S")
+            stage1(0, 1, 3)
+            h_out(1, 1, 0, "S")
+            stage1(1, 1, 2)
+            stage1(1, 0, 0)
+            x_out(2, 1, "S")
+            h_out(0, 1, 3, "S")
+            stage1(1, 1, 3)
+            h_inter(0, 1, "V")
+            h_out(1, 0, 0, "V")
+            x_quant(2)
+            h_quant(0, 1)
+            h_quant(0, 0)
+            w2_inter(1, 1, "S")
+            b2_spread()
+            turn(3, 0)
+            w2_quant(1)
+            h_out(1, 1, 3, "S")
+            h_out(1, 1, 2, "S")
+            stage1(1, 0, 3)
+            h_out(1, 0, 3, "S")
+            turn(3, 1)
+            stage1(2, 0, 1)
+            b2_out("S")
+            stage1(2, 0, 3)
+            x_out(3, 1, "S")
+            stage1(2, 1, 3)
+            h_out(2, 0, 3, "S")
+            h_out(2, 0, 1, "S")
+            h_inter(1, 1, "V")
+            h_inter(1, 0, "V")
+            x_out(3, 0, "S")
+            stage1(2, 1, 2)
+            h_out(2, 1, 3, "S")
+            stage2(0, 1)
+            v_bias(0, 1)
+            stage1(2, 0, 2)
+            x_quant(3)
+            h_out(2, 1, 2, "S")
+            stage1(2, 1, 0)
+            h_out(2, 1, 0, "S")
+            stage2(0, 0)
+            h_quant(1, 0)
+            stage1(2, 0, 0)
+            stage1(2, 1, 1)
+            h_quant(1, 1)
+            h_out(2, 0, 2, "S")
+            h_out(2, 0, 0, "S")
+            v_square(0, 1)
+            stage1(3, 1, 3)
+            stage1(3, 0, 1)
+            v_bias(0, 0)
+            h_out(2, 1, 1, "S")
+            stage2(1, 0)
+            stage1(3, 0, 0)
+            h_inter(2, 0, "V")
+            h_inter(2, 1, "V")
+            h_out(3, 1, 3, "S")
+            v_bias(1, 0)
+            stage1(3, 1, 0)
+            h_quant(2, 1)
+            stage2(1, 1)
+            v_square(0, 0)
+            h_out(3, 0, 1, "S")
+            stage1(3, 1, 2)
+            stage1(3, 0, 3)
+            h_quant(2, 0)
+            h_out(3, 0, 0, "S")
+            h_out(3, 1, 0, "S")
+            v_bias(1, 1)
+            stage1(3, 1, 1)
+            stage1(3, 0, 2)
+            v_square(1, 0)
+            h_out(3, 1, 2, "V")
+            stage2(2, 0)
+            h_out(3, 0, 3, "S")
+            h_out(3, 0, 2, "S")
+            v_bias(2, 0)
+            v_root(0)
+            v_max(0)
+            h_out(3, 1, 1, "S")
+            stage2(2, 1)
+            h_inter(3, 0, "S")
+            h_inter(3, 1, "V")
+            v_square(1, 1)
+            v_square(2, 0)
+            v_bias(2, 1)
+            v_recip(0)
+            h_quant(3, 1)
+            h_quant(3, 0)
+            stage2(3, 0)
+            stage2(3, 1)
+            v_mul(0, 0, "V")
+            v_root(1)
+            v_max(1)
+            v_mul(0, 1, "V")
+            v_square(2, 1)
+            v_recip(1)
+            v_root(2)
+            v_store(0, 0)
+            v_mul(1, 0, "S")
+            v_bias(3, 0)
+            v_square(3, 0)
+            v_bias(3, 1)
+            v_max(2)
+            v_mul(1, 1, "V")
+            v_square(3, 1)
+            v_store(0, 1)
+            v_store(1, 0)
+            v_root(3)
+            v_recip(2)
+            v_mul(2, 1, "V")
+            v_max(3)
+            v_store(1, 1)
+            v_recip(3)
+            v_mul(2, 0, "S")
+            v_store(2, 1)
+            v_store(2, 0)
+            v_mul(3, 1, "V")
+            v_store(3, 1)
+            v_mul(3, 0, "S")
+            v_store(3, 0)

@@ -25,7 +25,7 @@ def tile_geometricmanifoldnetwork_pa_kernel(tc, x_bytes, x_scale, W1, b1, W2, b2
     nc = tc.nc
     with ExitStack() as ctx:
         keep = ctx.enter_context(tc.tile_pool(name="keep", bufs=1))
-        work = ctx.enter_context(tc.tile_pool(name="work", bufs=4))
+        work = ctx.enter_context(tc.tile_pool(name="work", bufs=8))
         ps_x = ctx.enter_context(tc.psum_pool(name="ps_x", bufs=2))
         ps_h = ctx.enter_context(tc.psum_pool(name="ps_h", bufs=4))
         ps_o = ctx.enter_context(tc.psum_pool(name="ps_o", bufs=2))
@@ -37,19 +37,18 @@ def tile_geometricmanifoldnetwork_pa_kernel(tc, x_bytes, x_scale, W1, b1, W2, b2
         ident = keep.tile([P, P], F32, name="ident")
         make_identity(nc, ident[:])
         ident_b = keep.tile([P, P], BF16, name="ident_b")
-        make_identity(nc, ident_b[:])
+        nc.vector.tensor_copy(out=ident_b[:], in_=ident[:])
         one = keep.tile([P, 1], F32, name="one")
         nc.vector.memset(one[:], 1.0)
-        eps = keep.tile([P, 1], F32, name="eps")
-        nc.scalar.activation(out=eps[:], in_=one[:], func=ACT.Sqrt, scale=EPS * EPS)
+        top = keep.tile([P, 1], F32, name="top")
+        nc.scalar.activation(out=top[:], in_=one[:], func=ACT.Abs_reciprocal_sqrt, scale=EPS * EPS)
         nchunk = [(b - a) * P for a, b in CHUNKS]
 
         s_col = keep.tile([P, 8], F32, name="s_col")
         b1_col = keep.tile([P, 2, 4], BF16, name="b1_col")
-        b2_col = keep.tile([P, 4], BF16, name="b2_col")
         s_all = keep.tile([P, 128, 8], F32, name="s_all")
         s_flat = s_all[:].rearrange("q p c -> q (p c)")
-        b2_all = keep.tile([P, OUT], F32, name="b2_all")
+        b2_all = keep.tile([P, OUT], BF16, name="b2_all")
         T = {}
 
         def load_s():
@@ -57,15 +56,18 @@ def tile_geometricmanifoldnetwork_pa_kernel(tc, x_bytes, x_scale, W1, b1, W2, b2
 
         def load_b():
             nc.sync.dma_start(out=b1_col[:], in_=b1.rearrange("(g p t) -> p g t", p=P, t=4))
-            nc.sync.dma_start(out=b2_col[:], in_=b2.rearrange("(p c) -> p c", c=4))
 
-        def load_w1(g, G):
-            t = keep.tile([P, 4, 512], BF16, name=f"w1_raw_{g}_{G}")
+        def load_b2():
+            nc.sync.dma_start(out=b2_all[:], in_=b2.partition_broadcast(P))
+
+        def load_w1(g, G, h0, h1):
+            c0, c1 = 512 * G + 256 * h0, 512 * G + 256 * h1
+            t = keep.tile([P, 4, c1 - c0], BF16, name=f"w1_raw_{g}_{G}_{h0}")
             nc.sync.dma_start(
-                out=t[:],
-                in_=W1[512 * g : 512 * g + 512, 512 * G : 512 * G + 512].rearrange("(p j) c -> p j c", j=4),
+                out=t[:], in_=W1[512 * g : 512 * g + 512, c0:c1].rearrange("(p j) c -> p j c", j=4)
             )
-            T["w1_raw", g, G] = t
+            for h in range(h0, h1):
+                T["w1_raw", g, G, h] = t[:, :, 256 * (h - h0) : 256 * (h - h0) + 256]
 
         def load_x(c):
             n0, n1 = CHUNKS[c]
@@ -98,13 +100,33 @@ def tile_geometricmanifoldnetwork_pa_kernel(tc, x_bytes, x_scale, W1, b1, W2, b2
         def s_out(h, eng):
             copy(eng, s_all[:, :, 4 * h : 4 * h + 4], T["s_bank", h][:].rearrange("q c p -> q p c"))
 
+        def w1_turn(g, G, h):
+            bank = ps_h.tile([P, 1024], BF16, name="bank_h")
+            view = bank[:].rearrange("p (t m j) -> p j m t", t=4, j=4)
+            src = T["w1_raw", g, G, h].rearrange("p j (m t) -> p j m t", t=4)
+            for q in range(2):
+                m = slice(32 * q, 32 * q + 32)
+                nc.tensor.matmul(view[:, :, m, :], lhsT=ident_b[:], rhs=src[:, :, m, :], start=True, stop=True)
+            T["w1_bank", g, G, h] = bank
+
         def w1_inter(g, G, h, eng):
             if ("w1_grp", g, G) not in T:
                 T["w1_grp", g, G] = keep.tile([P, 2048], BF16, name=f"w1_grp_{g}_{G}", align_bytes=64)
-            m = slice(64 * h, 64 * h + 64)
-            dst = T["w1_grp", g, G][:].rearrange("p (t m j) -> p m j t", t=4, j=4)[:, m]
-            src = T["w1_raw", g, G][:].rearrange("p j (m t) -> p m j t", t=4)[:, m]
-            copy(eng, dst, src)
+            if ("w1_bank", g, G, h) in T:
+                dst = T["w1_grp", g, G][:].rearrange("p (t r) -> p t r", t=4)[:, :, 256 * h : 256 * h + 256]
+                copy(eng, dst, T["w1_bank", g, G, h][:].rearrange("p (t r) -> p t r", t=4))
+            else:
+                dst = T["w1_grp", g, G][:].rearrange("p (t m j) -> p m j t", t=4, j=4)[:, 64 * h : 64 * h + 64]
+                copy(eng, dst, T["w1_raw", g, G, h].rearrange("p j (m t) -> p m j t", t=4))
+
+        def w2_turn(G, h):
+            bank = ps_h.tile([P, 1024], BF16, name="bank_h")
+            view = bank[:].rearrange("p (c j) -> p j c", j=4)
+            for q in range(2):
+                c = slice(128 * q, 128 * q + 128)
+                src = T["w2_raw", G][:, :, 256 * h + 128 * q : 256 * h + 128 * q + 128]
+                nc.tensor.matmul(view[:, :, c], lhsT=ident_b[:], rhs=src, start=True, stop=True)
+            T["w2_bank", G, h] = bank
 
         def quantize(key, words, src):
             code = keep.tile([P, words], U32, name="code_" + key, align_bytes=64)
@@ -119,6 +141,9 @@ def tile_geometricmanifoldnetwork_pa_kernel(tc, x_bytes, x_scale, W1, b1, W2, b2
             if ("w2_grp", G) not in T:
                 T["w2_grp", G] = keep.tile([P, 512, 4], BF16, name=f"w2_grp_{G}", align_bytes=64)
             c = slice(256 * h, 256 * h + 256)
+            if ("w2_bank", G, h) in T:
+                copy(eng, T["w2_grp", G][:, c, :].rearrange("p c t -> p (c t)"), T["w2_bank", G, h][:])
+                return
             dst = T["w2_grp", G][:, c, :].rearrange("p (c i) t -> p c t i", i=4)
             src = T["w2_raw", G][:, :, c].rearrange("p t (c i) -> p c t i", i=4)
             copy(eng, dst, src)
@@ -189,17 +214,6 @@ def tile_geometricmanifoldnetwork_pa_kernel(tc, x_bytes, x_scale, W1, b1, W2, b2
         def h_quant(c, G):
             T["h", c, G] = quantize(f"h_{c}_{G}", nchunk[c], T["h_grp", c, G][:].rearrange("p n t -> p (n t)"))
 
-        def b2_spread():
-            bank = ps_o.tile([P, 4, P], F32, name="bank_o")
-            for c in range(4):
-                nc.tensor.matmul(
-                    bank[:, c, :], lhsT=b2_col[:, c : c + 1].to_broadcast([P, P]), rhs=ident_b[:], start=True, stop=True
-                )
-            T["b2_bank"] = bank
-
-        def b2_out(eng):
-            copy(eng, b2_all[:].rearrange("q (p c) -> q p c", c=4), T["b2_bank"][:].rearrange("q c p -> q p c"))
-
         def stage2(c, i):
             bank = ps_o.tile([P, OUT], F32, name="bank_o")
             for G in range(2):
@@ -229,226 +243,223 @@ def tile_geometricmanifoldnetwork_pa_kernel(tc, x_bytes, x_scale, W1, b1, W2, b2
 
         def v_root(c):
             T["nrm", c] = keep.tile([P, nchunk[c] // P], F32, name=f"nrm_{c}")
-            nc.scalar.activation(out=T["nrm", c][:], in_=T["ss", c][:], func=ACT.Sqrt)
+            nc.scalar.activation(out=T["nrm", c][:], in_=T["ss", c][:], func=ACT.Abs_reciprocal_sqrt)
 
         def v_max(c):
-            T["mx", c] = keep.tile([P, nchunk[c] // P], F32, name=f"mx_{c}")
+            T["rn", c] = keep.tile([P, nchunk[c] // P], F32, name=f"rn_{c}")
             nc.vector.tensor_scalar(
-                out=T["mx", c][:], in0=T["nrm", c][:], scalar1=eps[:, 0:1], scalar2=None, op0=ALU.max
+                out=T["rn", c][:], in0=T["nrm", c][:], scalar1=top[:, 0:1], scalar2=None, op0=ALU.min
             )
 
-        def v_recip(c):
-            T["rn", c] = keep.tile([P, nchunk[c] // P], F32, name=f"rn_{c}")
-            nc.vector.reciprocal(out=T["rn", c][:], in_=T["mx", c][:])
-
         def v_mul(c, i, eng):
-            t = keep.tile([P, OUT], F32, name=f"res_{c}_{i}")
+            if ("res", c) not in T:
+                T["res", c] = keep.tile([P, nchunk[c] // P, OUT], F32, name=f"res_{c}")
+            t = T["res", c][:, i, :]
             r = T["rn", c][:, i : i + 1]
             v = T["v", c, i][:]
             if eng == "V":
-                nc.vector.tensor_scalar(out=t[:], in0=v, scalar1=r, scalar2=None, op0=ALU.mult)
+                nc.vector.tensor_scalar(out=t, in0=v, scalar1=r, scalar2=None, op0=ALU.mult)
             elif eng == "S":
-                nc.scalar.activation(out=t[:], in_=v, func=ACT.Copy, scale=r)
+                nc.scalar.activation(out=t, in_=v, func=ACT.Copy, scale=r)
             else:
-                nc.gpsimd.tensor_scalar(out=t[:], in0=v, scalar1=r, scalar2=1.0, op0=ALU.mult, op1=ALU.mult)
-            T["res", c, i] = t
+                nc.gpsimd.tensor_scalar(out=t, in0=v, scalar1=r, scalar2=1.0, op0=ALU.mult, op1=ALU.mult)
 
-        def v_store(c, i):
-            nc.sync.dma_start(out=out_view[:, CHUNKS[c][0] + i, :], in_=T["res", c, i][:])
+        def v_store(c, i0, i1):
+            n0 = CHUNKS[c][0]
+            nc.sync.dma_start(out=out_view[:, n0 + i0 : n0 + i1, :], in_=T["res", c][:, i0:i1, :])
 
         with tc.manual_schedule():
             load_s()
-            load_x(0)
+            load_w1(0, 0, 1, 2)
             s_turn()
-            load_w1(0, 0)
-            s_out(0, "S")
-            load_w1(1, 1)
-            s_out(1, "V")
+            w1_turn(0, 0, 1)
+            s_out(1, "S")
+            load_x(0)
+            load_w1(0, 0, 0, 1)
+            w1_turn(0, 0, 0)
+            s_out(0, "V")
             load_x(2)
             prod(0, 1)
-            prod(0, 0)
-            load_x(1)
-            w1_inter(1, 1, 1, "V")
+            w1_inter(0, 0, 1, "S")
+            load_w1(1, 0, 0, 2)
             turn(0, 1)
             w1_inter(0, 0, 0, "S")
-            w1_inter(0, 0, 1, "S")
-            load_w1(1, 0)
-            prod(1, 1)
-            w1_inter(1, 1, 0, "S")
-            load_w1(0, 1)
-            w1_inter(1, 0, 1, "S")
             prod(2, 0)
-            turn(0, 0)
-            w1_quant(0, 0)
-            w1_inter(0, 1, 1, "S")
-            prod(1, 0)
             x_out(0, 1, "S")
-            x_out(0, 0, "S")
-            w1_inter(1, 0, 0, "S")
-            turn(1, 0)
-            x_out(1, 0, "S")
-            w1_inter(0, 1, 0, "V")
-            load_w2(0)
-            turn(1, 1)
-            x_quant(0)
-            prod(2, 1)
-            x_out(1, 1, "S")
-            w1_quant(1, 0)
-            w2_inter(0, 0, "S")
-            w1_quant(0, 1)
             turn(2, 0)
-            load_b()
-            stage1(0, 0, 3)
-            stage1(0, 0, 0)
-            x_quant(1)
-            stage1(0, 0, 1)
-            load_x(3)
-            h_out(0, 0, 3, "V")
-            h_out(0, 0, 0, "S")
-            w1_quant(1, 1)
-            stage1(0, 0, 2)
             x_out(2, 0, "S")
-            stage1(1, 0, 2)
-            h_out(1, 0, 2, "V")
-            stage1(1, 0, 1)
-            h_out(0, 0, 2, "S")
-            load_w2(1)
+            load_w1(1, 1, 0, 2)
+            load_x(1)
+            w1_turn(1, 0, 1)
+            w1_inter(1, 0, 1, "S")
+            prod(0, 0)
+            w1_quant(0, 0)
+            prod(2, 1)
+            load_w1(0, 1, 0, 2)
+            w1_inter(1, 1, 1, "S")
+            w1_turn(1, 0, 0)
+            turn(0, 0)
+            w1_inter(1, 0, 0, "S")
+            w1_turn(1, 1, 0)
+            prod(1, 1)
+            prod(1, 0)
+            x_out(0, 0, "S")
+            w1_inter(1, 1, 0, "S")
+            load_b()
             turn(2, 1)
-            h_out(0, 0, 1, "S")
-            w2_inter(0, 1, "S")
-            stage1(1, 1, 1)
-            h_out(1, 0, 1, "S")
-            stage1(0, 1, 0)
-            h_out(1, 1, 1, "S")
-            stage1(0, 1, 1)
-            prod(3, 1)
-            w2_inter(1, 0, "V")
-            h_out(0, 1, 1, "V")
-            h_out(0, 1, 0, "S")
-            stage1(0, 1, 2)
-            h_inter(0, 0, "V")
-            stage1(1, 1, 0)
-            w2_quant(0)
-            prod(3, 0)
-            h_out(0, 1, 2, "S")
-            stage1(0, 1, 3)
-            h_out(1, 1, 0, "S")
-            stage1(1, 1, 2)
-            stage1(1, 0, 0)
+            w1_turn(0, 1, 0)
+            w1_quant(1, 0)
             x_out(2, 1, "S")
-            h_out(0, 1, 3, "S")
-            stage1(1, 1, 3)
-            h_inter(0, 1, "V")
-            h_out(1, 0, 0, "V")
+            load_x(3)
+            turn(1, 1)
+            w1_inter(0, 1, 1, "S")
+            x_quant(0)
+            turn(1, 0)
+            w1_inter(0, 1, 0, "S")
+            x_out(1, 1, "S")
+            load_w2(1)
+            stage1(0, 0, 3)
+            stage1(0, 0, 1)
+            prod(3, 0)
             x_quant(2)
-            h_quant(0, 1)
-            h_quant(0, 0)
-            w2_inter(1, 1, "S")
-            b2_spread()
+            h_out(0, 0, 3, "S")
+            stage1(0, 0, 2)
             turn(3, 0)
-            w2_quant(1)
-            h_out(1, 1, 3, "S")
-            h_out(1, 1, 2, "S")
-            stage1(1, 0, 3)
-            h_out(1, 0, 3, "S")
-            turn(3, 1)
-            stage1(2, 0, 1)
-            b2_out("S")
+            stage1(0, 0, 0)
+            w1_quant(1, 1)
+            load_w2(0)
+            h_out(0, 0, 1, "S")
+            w1_quant(0, 1)
+            x_out(1, 0, "S")
+            h_out(0, 0, 2, "S")
+            h_out(0, 0, 0, "S")
             stage1(2, 0, 3)
-            x_out(3, 1, "S")
-            stage1(2, 1, 3)
+            stage1(0, 1, 3)
             h_out(2, 0, 3, "S")
-            h_out(2, 0, 1, "S")
-            h_inter(1, 1, "V")
-            h_inter(1, 0, "V")
-            x_out(3, 0, "S")
-            stage1(2, 1, 2)
-            h_out(2, 1, 3, "S")
-            stage2(0, 1)
-            v_bias(0, 1)
             stage1(2, 0, 2)
-            x_quant(3)
-            h_out(2, 1, 2, "S")
-            stage1(2, 1, 0)
-            h_out(2, 1, 0, "S")
-            stage2(0, 0)
-            h_quant(1, 0)
+            prod(3, 1)
+            x_out(3, 0, "S")
+            h_out(0, 1, 3, "S")
+            stage1(0, 1, 2)
+            w2_inter(1, 0, "V")
+            w2_inter(0, 1, "V")
+            x_quant(1)
+            w2_inter(0, 0, "V")
+            h_out(2, 0, 2, "S")
+            w2_inter(1, 1, "V")
             stage1(2, 0, 0)
+            turn(3, 1)
+            h_out(0, 1, 2, "S")
+            stage1(0, 1, 0)
+            stage1(1, 1, 0)
+            h_inter(0, 0, "V")
+            stage1(1, 0, 3)
+            h_out(2, 0, 0, "S")
+            x_out(3, 1, "S")
+            h_out(0, 1, 0, "S")
+            stage1(0, 1, 1)
+            h_out(1, 1, 0, "S")
+            stage1(1, 1, 3)
+            h_out(1, 0, 3, "S")
+            stage1(1, 0, 1)
+            h_out(0, 1, 1, "S")
+            h_out(1, 1, 3, "S")
+            h_out(1, 0, 1, "S")
+            stage1(1, 1, 1)
+            stage1(1, 0, 0)
+            w2_quant(1)
+            w2_quant(0)
+            stage1(1, 1, 2)
+            h_inter(0, 1, "V")
+            h_out(1, 1, 1, "S")
+            h_out(1, 0, 0, "S")
+            stage1(2, 1, 2)
+            h_quant(0, 0)
+            load_b2()
+            stage1(1, 0, 2)
+            stage1(2, 1, 3)
+            h_out(1, 1, 2, "S")
+            h_out(2, 1, 2, "S")
+            h_quant(0, 1)
+            h_inter(1, 1, "V")
+            h_out(1, 0, 2, "S")
+            stage1(2, 1, 0)
+            h_out(2, 1, 3, "S")
+            h_out(2, 1, 0, "S")
+            stage1(2, 0, 1)
+            stage2(0, 0)
+            h_out(2, 0, 1, "S")
+            x_quant(3)
+            stage2(0, 1)
             stage1(2, 1, 1)
             h_quant(1, 1)
-            h_out(2, 0, 2, "S")
-            h_out(2, 0, 0, "S")
-            v_square(0, 1)
-            stage1(3, 1, 3)
-            stage1(3, 0, 1)
-            v_bias(0, 0)
-            h_out(2, 1, 1, "S")
-            stage2(1, 0)
-            stage1(3, 0, 0)
+            h_inter(1, 0, "S")
             h_inter(2, 0, "V")
-            h_inter(2, 1, "V")
-            h_out(3, 1, 3, "S")
-            v_bias(1, 0)
-            stage1(3, 1, 0)
-            h_quant(2, 1)
-            stage2(1, 1)
-            v_square(0, 0)
-            h_out(3, 0, 1, "S")
-            stage1(3, 1, 2)
-            stage1(3, 0, 3)
-            h_quant(2, 0)
-            h_out(3, 0, 0, "S")
-            h_out(3, 1, 0, "S")
-            v_bias(1, 1)
+            h_out(2, 1, 1, "S")
+            stage1(3, 0, 1)
             stage1(3, 1, 1)
+            v_bias(0, 0)
+            h_out(3, 0, 1, "S")
+            stage1(3, 1, 3)
             stage1(3, 0, 2)
-            v_square(1, 0)
-            h_out(3, 1, 2, "V")
-            stage2(2, 0)
-            h_out(3, 0, 3, "S")
-            h_out(3, 0, 2, "S")
-            v_bias(2, 0)
-            v_root(0)
-            v_max(0)
+            h_quant(1, 0)
+            stage2(1, 0)
+            v_bias(0, 1)
+            stage2(1, 1)
             h_out(3, 1, 1, "S")
-            stage2(2, 1)
-            h_inter(3, 0, "S")
-            h_inter(3, 1, "V")
+            h_quant(2, 0)
+            v_square(0, 0)
+            stage1(3, 0, 0)
+            v_square(0, 1)
+            h_out(3, 1, 3, "S")
+            stage1(3, 0, 3)
+            h_inter(2, 1, "V")
+            h_out(3, 0, 2, "S")
+            v_root(0)
+            stage1(3, 1, 0)
+            stage1(3, 1, 2)
+            v_bias(1, 0)
+            v_bias(1, 1)
+            v_max(0)
+            h_quant(2, 1)
+            h_out(3, 0, 0, "S")
+            h_out(3, 0, 3, "S")
+            h_out(3, 1, 0, "S")
+            h_out(3, 1, 2, "S")
+            v_square(1, 0)
             v_square(1, 1)
-            v_square(2, 0)
-            v_bias(2, 1)
-            v_recip(0)
-            h_quant(3, 1)
-            h_quant(3, 0)
-            stage2(3, 0)
-            stage2(3, 1)
             v_mul(0, 0, "V")
+            h_inter(3, 0, "V")
             v_root(1)
+            h_inter(3, 1, "V")
+            h_quant(3, 0)
+            stage2(2, 0)
+            v_mul(0, 1, "S")
+            stage2(2, 1)
+            v_store(0, 0, 2)
+            h_quant(3, 1)
             v_max(1)
-            v_mul(0, 1, "V")
-            v_square(2, 1)
-            v_recip(1)
-            v_root(2)
-            v_store(0, 0)
-            v_mul(1, 0, "S")
+            v_bias(2, 0)
+            stage2(3, 0)
+            v_mul(1, 1, "S")
+            v_bias(2, 1)
+            v_mul(1, 0, "V")
+            v_square(2, 0)
             v_bias(3, 0)
-            v_square(3, 0)
+            stage2(3, 1)
+            v_store(1, 0, 2)
+            v_square(2, 1)
+            v_root(2)
             v_bias(3, 1)
-            v_max(2)
-            v_mul(1, 1, "V")
+            v_square(3, 0)
             v_square(3, 1)
-            v_store(0, 1)
-            v_store(1, 0)
             v_root(3)
-            v_recip(2)
+            v_max(2)
             v_mul(2, 1, "V")
+            v_mul(2, 0, "V")
             v_max(3)
-            v_store(1, 1)
-            v_recip(3)
-            v_mul(2, 0, "S")
-            v_store(2, 1)
-            v_store(2, 0)
+            v_store(2, 0, 2)
             v_mul(3, 1, "V")
-            v_store(3, 1)
-            v_mul(3, 0, "S")
-            v_store(3, 0)
+            v_store(3, 1, 2)
+            v_mul(3, 0, "V")
+            v_store(3, 0, 1)

from contextlib import ExitStack

import concourse.mybir as mybir
from concourse.masks import make_identity

B, IN, F, OUT = 1024, 1024, 1024, 512
FLOPS = 2 * B * IN * F + 2 * B * F * OUT
EPS = 1e-12

F32 = mybir.dt.float32
BF16 = mybir.dt.bfloat16
U32 = mybir.dt.uint32
U8 = mybir.dt.uint8
FP8 = mybir.dt.float8_e4m3fn
FP8X4 = mybir.dt.float8_e4m3fn_x4
ACT = mybir.ActivationFunctionType
ALU = mybir.AluOpType

P = 128
NT = 8
CHUNKS = [(0, 2), (2, 4), (4, 6), (6, 8)]


def tile_geometricmanifoldnetwork_pa_kernel(tc, x_bytes, x_scale, W1, b1, W2, b2, out):
    nc = tc.nc
    with ExitStack() as ctx:
        keep = ctx.enter_context(tc.tile_pool(name="keep", bufs=1))
        work = ctx.enter_context(tc.tile_pool(name="work", bufs=8))
        ps_x = ctx.enter_context(tc.psum_pool(name="ps_x", bufs=2))
        ps_h = ctx.enter_context(tc.psum_pool(name="ps_h", bufs=4))
        ps_o = ctx.enter_context(tc.psum_pool(name="ps_o", bufs=2))

        x_view = x_bytes.rearrange("(p n) k -> p n k", n=NT)
        out_view = out.rearrange("(p n) m -> p n m", n=NT)


        ident = keep.tile([P, P], F32, name="ident")
        make_identity(nc, ident[:])
        ident_b = keep.tile([P, P], BF16, name="ident_b")
        nc.vector.tensor_copy(out=ident_b[:], in_=ident[:])
        one = keep.tile([P, 1], F32, name="one")
        nc.vector.memset(one[:], 1.0)
        top = keep.tile([P, 1], F32, name="top")
        nc.scalar.activation(out=top[:], in_=one[:], func=ACT.Abs_reciprocal_sqrt, scale=EPS * EPS)
        nchunk = [(b - a) * P for a, b in CHUNKS]

        s_col = keep.tile([P, 8], F32, name="s_col")
        b1_col = keep.tile([P, 2, 4], BF16, name="b1_col")
        s_all = keep.tile([P, 128, 8], F32, name="s_all")
        s_flat = s_all[:].rearrange("q p c -> q (p c)")
        b2_all = keep.tile([P, OUT], BF16, name="b2_all")
        T = {}

        def load_s():
            nc.sync.dma_start(out=s_col[:], in_=x_scale.rearrange("o (p c) -> p (o c)", c=8))

        def load_b():
            nc.sync.dma_start(out=b1_col[:], in_=b1.rearrange("(g p t) -> p g t", p=P, t=4))

        def load_b2():
            nc.sync.dma_start(out=b2_all[:], in_=b2.partition_broadcast(P))

        def load_w1(g, G, h0, h1):
            c0, c1 = 512 * G + 256 * h0, 512 * G + 256 * h1
            t = keep.tile([P, 4, c1 - c0], BF16, name=f"w1_raw_{g}_{G}_{h0}")
            nc.sync.dma_start(
                out=t[:], in_=W1[512 * g : 512 * g + 512, c0:c1].rearrange("(p j) c -> p j c", j=4)
            )
            for h in range(h0, h1):
                T["w1_raw", g, G, h] = t[:, :, 256 * (h - h0) : 256 * (h - h0) + 256]

        def load_x(c):
            n0, n1 = CHUNKS[c]
            t = keep.tile([P, n1 - n0, IN], U8, name=f"x_raw_{c}")
            nc.sync.dma_start(out=t[:], in_=x_view[:, n0:n1, :])
            T["x_raw", c] = t

        def load_w2(G):
            t = keep.tile([P, 4, 512], BF16, name=f"w2_raw_{G}")
            nc.sync.dma_start(out=t[:], in_=W2[512 * G : 512 * G + 512, :].rearrange("(p j) c -> p j c", j=4))
            T["w2_raw", G] = t

        def copy(eng, dst, src):
            if eng == "V":
                nc.vector.tensor_copy(out=dst, in_=src)
            elif eng == "S":
                nc.scalar.copy(out=dst, in_=src)
            else:
                nc.gpsimd.tensor_scalar(out=dst, in0=src, scalar1=1.0, scalar2=0.0, op0=ALU.mult, op1=ALU.add)

        def s_turn():
            for h in range(2):
                bank = ps_x.tile([P, 4, P], F32, name="bank_x")
                for c in range(4):
                    nc.tensor.transpose(
                        bank[:, c, :], s_col[:, 4 * h + c : 4 * h + c + 1].to_broadcast([P, P]), ident[:]
                    )
                T["s_bank", h] = bank

        def s_out(h, eng):
            copy(eng, s_all[:, :, 4 * h : 4 * h + 4], T["s_bank", h][:].rearrange("q c p -> q p c"))

        def w1_turn(g, G, h):
            bank = ps_h.tile([P, 1024], BF16, name="bank_h")
            view = bank[:].rearrange("p (t m j) -> p j m t", t=4, j=4)
            src = T["w1_raw", g, G, h].rearrange("p j (m t) -> p j m t", t=4)
            for q in range(2):
                m = slice(32 * q, 32 * q + 32)
                nc.tensor.matmul(view[:, :, m, :], lhsT=ident_b[:], rhs=src[:, :, m, :], start=True, stop=True)
            T["w1_bank", g, G, h] = bank

        def w1_inter(g, G, h, eng):
            if ("w1_grp", g, G) not in T:
                T["w1_grp", g, G] = keep.tile([P, 2048], BF16, name=f"w1_grp_{g}_{G}", align_bytes=64)
            if ("w1_bank", g, G, h) in T:
                dst = T["w1_grp", g, G][:].rearrange("p (t r) -> p t r", t=4)[:, :, 256 * h : 256 * h + 256]
                copy(eng, dst, T["w1_bank", g, G, h][:].rearrange("p (t r) -> p t r", t=4))
            else:
                dst = T["w1_grp", g, G][:].rearrange("p (t m j) -> p m j t", t=4, j=4)[:, 64 * h : 64 * h + 64]
                copy(eng, dst, T["w1_raw", g, G, h].rearrange("p j (m t) -> p m j t", t=4))

        def w2_turn(G, h):
            bank = ps_h.tile([P, 1024], BF16, name="bank_h")
            view = bank[:].rearrange("p (c j) -> p j c", j=4)
            for q in range(2):
                c = slice(128 * q, 128 * q + 128)
                src = T["w2_raw", G][:, :, 256 * h + 128 * q : 256 * h + 128 * q + 128]
                nc.tensor.matmul(view[:, :, c], lhsT=ident_b[:], rhs=src, start=True, stop=True)
            T["w2_bank", G, h] = bank

        def quantize(key, words, src):
            code = keep.tile([P, words], U32, name="code_" + key, align_bytes=64)
            scl = keep.tile([P, words], U8, name="scl_" + key, align_bytes=64)
            nc.vector.quantize_mx(out=code[:].bitcast(FP8X4), scales=scl[:], in_=src)
            return code, scl

        def w1_quant(g, G):
            T["w1", g, G] = quantize(f"w1_{g}_{G}", 512, T["w1_grp", g, G][:])

        def w2_inter(G, h, eng):
            if ("w2_grp", G) not in T:
                T["w2_grp", G] = keep.tile([P, 512, 4], BF16, name=f"w2_grp_{G}", align_bytes=64)
            c = slice(256 * h, 256 * h + 256)
            if ("w2_bank", G, h) in T:
                copy(eng, T["w2_grp", G][:, c, :].rearrange("p c t -> p (c t)"), T["w2_bank", G, h][:])
                return
            dst = T["w2_grp", G][:, c, :].rearrange("p (c i) t -> p c t i", i=4)
            src = T["w2_raw", G][:, :, c].rearrange("p t (c i) -> p c t i", i=4)
            copy(eng, dst, src)

        def w2_quant(G):
            T["w2", G] = quantize(f"w2_{G}", 512, T["w2_grp", G][:].rearrange("p c t -> p (c t)"))

        def prod(c, i):
            t = work.tile([P, IN], BF16, name="x_prod")
            nc.vector.tensor_tensor(out=t[:], in0=T["x_raw", c][:, i, :].bitcast(FP8), in1=s_flat, op=ALU.mult)
            T["x_prod", c, i] = t

        def turn(c, i):
            words = T["x_prod", c, i][:].bitcast(F32)
            bank = ps_x.tile([P, 2, 2, P], F32, name="bank_x")
            for g in range(2):
                for u in range(2):
                    nc.tensor.transpose(bank[:, g, u, :], words[:, 256 * g + u : 256 * g + 256 : 2], ident[:])
            T["x_bank", c, i] = bank

        def x_out(c, i, eng):
            if ("x_grp", c) not in T:
                T["x_grp", c] = keep.tile([P, 2, nchunk[c], 4], BF16, name=f"x_grp_{c}", align_bytes=64)
            dst = T["x_grp", c][:, :, P * i : P * i + P, :].bitcast(F32)
            copy(eng, dst, T["x_bank", c, i][:].rearrange("p g u r -> p g r u"))

        def x_quant(c):
            T["x", c] = quantize(f"x_{c}", 2 * nchunk[c], T["x_grp", c][:].rearrange("p g n t -> p (g n t)"))

        def stage1(c, G, t):
            n = nchunk[c]
            bank = ps_h.tile([P, 512], F32, name="bank_h")
            for g in range(2):
                w_code, w_scl = T["w1", g, G]
                x_code, x_scl = T["x", c]
                nc.tensor.matmul_mx(
                    out=bank[:, :n],
                    lhsT=w_code[:, P * t : P * t + P].bitcast(FP8X4),
                    lhsT_scale=w_scl[:, P * t : P * t + P],
                    rhs=x_code[:, g * n : g * n + n].bitcast(FP8X4),
                    rhs_scale=x_scl[:, g * n : g * n + n],
                    start=(g == 0),
                    stop=(g == 1),
                )
            T["h_bank", c, G, t] = bank

        def h_out(c, G, t, eng):
            n = nchunk[c]
            if ("h_plane", c, G) not in T:
                T["h_plane", c, G] = work.tile([P, 4, n], BF16, name=f"h_plane_{n}")
            dst = T["h_plane", c, G][:, t, :]
            src = T["h_bank", c, G, t][:, :n]
            bias = b1_col[:, G, t : t + 1]
            if eng == "S":
                nc.scalar.activation(out=dst, in_=src, func=ACT.Relu, bias=bias)
            else:
                nc.vector.tensor_scalar(out=dst, in0=src, scalar1=bias, scalar2=0.0, op0=ALU.add, op1=ALU.max)

        def h_inter(c, G, eng):
            t = work.tile([P, nchunk[c], 4], BF16, name=f"h_grp_{nchunk[c]}", align_bytes=64)
            copy(
                eng,
                t[:].rearrange("p (c i) t -> p c t i", i=4),
                T["h_plane", c, G][:].rearrange("p t (c i) -> p c t i", i=4),
            )
            T["h_grp", c, G] = t

        def h_quant(c, G):
            T["h", c, G] = quantize(f"h_{c}_{G}", nchunk[c], T["h_grp", c, G][:].rearrange("p n t -> p (n t)"))

        def stage2(c, i):
            bank = ps_o.tile([P, OUT], F32, name="bank_o")
            for G in range(2):
                h_code, h_scl = T["h", c, G]
                w_code, w_scl = T["w2", G]
                nc.tensor.matmul_mx(
                    out=bank[:],
                    lhsT=h_code[:, P * i : P * i + P].bitcast(FP8X4),
                    lhsT_scale=h_scl[:, P * i : P * i + P],
                    rhs=w_code[:].bitcast(FP8X4),
                    rhs_scale=w_scl[:],
                    start=(G == 0),
                    stop=(G == 1),
                )
            T["o_bank", c, i] = bank

        def v_bias(c, i):
            t = keep.tile([P, OUT], F32, name=f"v_{c}_{i}")
            nc.vector.tensor_tensor(out=t[:], in0=T["o_bank", c, i][:], in1=b2_all[:], op=ALU.add)
            T["v", c, i] = t

        def v_square(c, i):
            if ("ss", c) not in T:
                T["ss", c] = keep.tile([P, nchunk[c] // P], F32, name=f"ss_{c}")
            junk = work.tile([P, OUT], BF16, name="junk")
            nc.scalar.activation(out=junk[:], in_=T["v", c, i][:], func=ACT.Square, accum_out=T["ss", c][:, i : i + 1])

        def v_root(c):
            T["nrm", c] = keep.tile([P, nchunk[c] // P], F32, name=f"nrm_{c}")
            nc.scalar.activation(out=T["nrm", c][:], in_=T["ss", c][:], func=ACT.Abs_reciprocal_sqrt)

        def v_max(c):
            T["rn", c] = keep.tile([P, nchunk[c] // P], F32, name=f"rn_{c}")
            nc.vector.tensor_scalar(
                out=T["rn", c][:], in0=T["nrm", c][:], scalar1=top[:, 0:1], scalar2=None, op0=ALU.min
            )

        def v_mul(c, i, eng):
            if ("res", c) not in T:
                T["res", c] = keep.tile([P, nchunk[c] // P, OUT], F32, name=f"res_{c}")
            t = T["res", c][:, i, :]
            r = T["rn", c][:, i : i + 1]
            v = T["v", c, i][:]
            if eng == "V":
                nc.vector.tensor_scalar(out=t, in0=v, scalar1=r, scalar2=None, op0=ALU.mult)
            elif eng == "S":
                nc.scalar.activation(out=t, in_=v, func=ACT.Copy, scale=r)
            else:
                nc.gpsimd.tensor_scalar(out=t, in0=v, scalar1=r, scalar2=1.0, op0=ALU.mult, op1=ALU.mult)

        def v_store(c, i0, i1):
            n0 = CHUNKS[c][0]
            nc.sync.dma_start(out=out_view[:, n0 + i0 : n0 + i1, :], in_=T["res", c][:, i0:i1, :])

        with tc.manual_schedule():
            load_s()
            load_w1(0, 0, 1, 2)
            s_turn()
            w1_turn(0, 0, 1)
            s_out(1, "S")
            load_x(0)
            load_w1(0, 0, 0, 1)
            w1_turn(0, 0, 0)
            s_out(0, "V")
            load_x(2)
            prod(0, 1)
            w1_inter(0, 0, 1, "S")
            load_w1(1, 0, 0, 2)
            turn(0, 1)
            w1_inter(0, 0, 0, "S")
            prod(2, 0)
            x_out(0, 1, "S")
            turn(2, 0)
            x_out(2, 0, "S")
            load_w1(1, 1, 0, 2)
            load_x(1)
            w1_turn(1, 0, 1)
            w1_inter(1, 0, 1, "S")
            prod(0, 0)
            w1_quant(0, 0)
            prod(2, 1)
            load_w1(0, 1, 0, 2)
            w1_inter(1, 1, 1, "S")
            w1_turn(1, 0, 0)
            turn(0, 0)
            w1_inter(1, 0, 0, "S")
            w1_turn(1, 1, 0)
            prod(1, 1)
            prod(1, 0)
            x_out(0, 0, "S")
            w1_inter(1, 1, 0, "S")
            load_b()
            turn(2, 1)
            w1_turn(0, 1, 0)
            w1_quant(1, 0)
            x_out(2, 1, "S")
            load_x(3)
            turn(1, 1)
            w1_inter(0, 1, 1, "S")
            x_quant(0)
            turn(1, 0)
            w1_inter(0, 1, 0, "S")
            x_out(1, 1, "S")
            load_w2(1)
            stage1(0, 0, 3)
            stage1(0, 0, 1)
            prod(3, 0)
            x_quant(2)
            h_out(0, 0, 3, "S")
            stage1(0, 0, 2)
            turn(3, 0)
            stage1(0, 0, 0)
            w1_quant(1, 1)
            load_w2(0)
            h_out(0, 0, 1, "S")
            w1_quant(0, 1)
            x_out(1, 0, "S")
            h_out(0, 0, 2, "S")
            h_out(0, 0, 0, "S")
            stage1(2, 0, 3)
            stage1(0, 1, 3)
            h_out(2, 0, 3, "S")
            stage1(2, 0, 2)
            prod(3, 1)
            x_out(3, 0, "S")
            h_out(0, 1, 3, "S")
            stage1(0, 1, 2)
            w2_inter(1, 0, "V")
            w2_inter(0, 1, "V")
            x_quant(1)
            w2_inter(0, 0, "V")
            h_out(2, 0, 2, "S")
            w2_inter(1, 1, "V")
            stage1(2, 0, 0)
            turn(3, 1)
            h_out(0, 1, 2, "S")
            stage1(0, 1, 0)
            stage1(1, 1, 0)
            h_inter(0, 0, "V")
            stage1(1, 0, 3)
            h_out(2, 0, 0, "S")
            x_out(3, 1, "S")
            h_out(0, 1, 0, "S")
            stage1(0, 1, 1)
            h_out(1, 1, 0, "S")
            stage1(1, 1, 3)
            h_out(1, 0, 3, "S")
            stage1(1, 0, 1)
            h_out(0, 1, 1, "S")
            h_out(1, 1, 3, "S")
            h_out(1, 0, 1, "S")
            stage1(1, 1, 1)
            stage1(1, 0, 0)
            w2_quant(1)
            w2_quant(0)
            stage1(1, 1, 2)
            h_inter(0, 1, "V")
            h_out(1, 1, 1, "S")
            h_out(1, 0, 0, "S")
            stage1(2, 1, 2)
            h_quant(0, 0)
            load_b2()
            stage1(1, 0, 2)
            stage1(2, 1, 3)
            h_out(1, 1, 2, "S")
            h_out(2, 1, 2, "S")
            h_quant(0, 1)
            h_inter(1, 1, "V")
            h_out(1, 0, 2, "S")
            stage1(2, 1, 0)
            h_out(2, 1, 3, "S")
            h_out(2, 1, 0, "S")
            stage1(2, 0, 1)
            stage2(0, 0)
            h_out(2, 0, 1, "S")
            x_quant(3)
            stage2(0, 1)
            stage1(2, 1, 1)
            h_quant(1, 1)
            h_inter(1, 0, "S")
            h_inter(2, 0, "V")
            h_out(2, 1, 1, "S")
            stage1(3, 0, 1)
            stage1(3, 1, 1)
            v_bias(0, 0)
            h_out(3, 0, 1, "S")
            stage1(3, 1, 3)
            stage1(3, 0, 2)
            h_quant(1, 0)
            stage2(1, 0)
            v_bias(0, 1)
            stage2(1, 1)
            h_out(3, 1, 1, "S")
            h_quant(2, 0)
            v_square(0, 0)
            stage1(3, 0, 0)
            v_square(0, 1)
            h_out(3, 1, 3, "S")
            stage1(3, 0, 3)
            h_inter(2, 1, "V")
            h_out(3, 0, 2, "S")
            v_root(0)
            stage1(3, 1, 0)
            stage1(3, 1, 2)
            v_bias(1, 0)
            v_bias(1, 1)
            v_max(0)
            h_quant(2, 1)
            h_out(3, 0, 0, "S")
            h_out(3, 0, 3, "S")
            h_out(3, 1, 0, "S")
            h_out(3, 1, 2, "S")
            v_square(1, 0)
            v_square(1, 1)
            v_mul(0, 0, "V")
            h_inter(3, 0, "V")
            v_root(1)
            h_inter(3, 1, "V")
            h_quant(3, 0)
            stage2(2, 0)
            v_mul(0, 1, "S")
            stage2(2, 1)
            v_store(0, 0, 2)
            h_quant(3, 1)
            v_max(1)
            v_bias(2, 0)
            stage2(3, 0)
            v_mul(1, 1, "S")
            v_bias(2, 1)
            v_mul(1, 0, "V")
            v_square(2, 0)
            v_bias(3, 0)
            stage2(3, 1)
            v_store(1, 0, 2)
            v_square(2, 1)
            v_root(2)
            v_bias(3, 1)
            v_square(3, 0)
            v_square(3, 1)
            v_root(3)
            v_max(2)
            v_mul(2, 1, "V")
            v_mul(2, 0, "V")
            v_max(3)
            v_store(2, 0, 2)
            v_mul(3, 1, "V")
            v_store(3, 1, 2)
            v_mul(3, 0, "V")
            v_store(3, 0, 1)
